import numpy as np
import ml_dtypes


def mxq(x, axis, fmt="e4m3"):
    dtype, down = {"e4m3": (ml_dtypes.float8_e4m3fn, 7), "e5m2": (ml_dtypes.float8_e5m2, 14)}[fmt]
    v = np.moveaxis(np.asarray(x, np.float32).astype(ml_dtypes.bfloat16).astype(np.float64), axis, -1)
    blocks = v.reshape(v.shape[:-1] + (-1, 32))
    amax = np.abs(blocks).max(-1, keepdims=True)
    byte = np.maximum(np.where(amax > 0, np.frexp(amax)[1] - 1 + 127, 0) - down, 1)
    scale = np.exp2(byte - 127.0)
    codes = (blocks / scale).astype(np.float32).astype(dtype).astype(np.float64)
    return np.moveaxis((codes * scale).reshape(v.shape), -1, axis)


WIDE = False


def mx_kscale(k):
    if not WIDE:
        return np.ones(k)
    levels = np.array([10, -10, 5, -5, 0])
    a = np.random.permutation(np.resize(levels, k // 512 * 4)).reshape(k // 512, 4)
    idx = np.arange(k)
    return np.exp2(a[idx // 512, idx % 128 // 32])


BF16 = ml_dtypes.bfloat16


def bf(x):
    return np.asarray(x, np.float32).astype(BF16)


def f64(x):
    return np.asarray(x).astype(np.float64)


B, S, D, E, F = 4, 64, 2048, 2048, 4096
EPS = 1e-5


def layernorm(x, g, b):
    m = x.mean(-1, keepdims=True)
    v = ((x - m) ** 2).mean(-1, keepdims=True)
    return (x - m) * (1.0 / np.sqrt(v + EPS)) * g + b


def rotate_half(x):
    return np.concatenate([-x[..., ::2], x[..., 1::2]], axis=-1)


def sinu_pos_emb(dim, length):
    inv_freq = 1.0 / 10000.0 ** (np.arange(0, dim, 2) / dim)
    sp = np.arange(length)[:, None] * inv_freq[None, :]
    return np.concatenate([np.sin(sp), np.cos(sp)], axis=-1)


def setup_inputs():
    s = mx_kscale(D)
    return {"src": bf(np.random.standard_normal((B, S, D)) + 0.5),
            "Wqkv": bf(np.random.standard_normal((3 * E, D)) / np.sqrt(D) / s[None, :]),
            "bqkv": bf(0.1 * np.random.standard_normal(3 * E)),
            "g1": bf((1.0 + 0.1 * np.random.standard_normal(D)) * s),
            "be1": bf(0.1 * np.random.standard_normal(D) * s)}


def reference(src, Wqkv, bqkv, g1, be1):
    xn = layernorm(f64(src), f64(g1), f64(be1))
    qkv = (mxq(xn, 2, "e4m3") @ mxq(f64(Wqkv), 1, "e4m3").T) + f64(bqkv)
    Q, K, V = qkv[..., :E], qkv[..., E:2 * E], qkv[..., 2 * E:]
    emb = sinu_pos_emb(E, S)
    c, s = np.cos(emb), np.sin(emb)
    Q = Q * c + rotate_half(Q) * s
    K = K * c - rotate_half(K) * s
    return Q, K, V

@@ -1,0 +1,274 @@
+import math
+from contextlib import ExitStack
+
+import concourse.mybir as mybir
+from concourse.masks import make_identity
+
+F32 = mybir.dt.float32
+BF16 = mybir.dt.bfloat16
+U32 = mybir.dt.uint32
+U8 = mybir.dt.uint8
+FP8X4 = mybir.dt.float8_e4m3fn_x4
+ALU = mybir.AluOpType
+ACT = mybir.ActivationFunctionType
+
+P = 128
+TOKENS = 256
+POSITIONS = 64
+TOKEN_TILES = TOKENS // P
+D = 2048
+E = 2048
+HALF_E = E // 2
+EPS = 1e-5
+
+PACK = 4
+K_PASS = P * PACK
+PASSES = D // K_PASS
+WORDS_PER_PASS = K_PASS // 2
+
+CHUNK = 512
+ROW_TILES = CHUNK // P
+CHUNKS = 3 * E // CHUNK
+CHUNKS_PER_OUTPUT = E // CHUNK
+UNITS = CHUNKS * PASSES
+UNITS_PER_RUN = 2
+
+ROUND = 1.5 * 2.0**23
+FREQ_RATIO = 10000.0 ** (-1.0 / HALF_E)
+
+FLOPS = 2 * TOKENS * D * 3 * E
+
+
+def tile_rotaryembeddingtransformerlayer_pa_kernel(
+    tc, src, Wqkv, bqkv, g1, be1, out_q, out_k, out_v
+):
+    nc = tc.nc
+    x_rows = src.flatten_outer_dims()
+    out_rows = [out_q.flatten_outer_dims(), out_k.flatten_outer_dims(), out_v.flatten_outer_dims()]
+
+    with ExitStack() as pools:
+        const = pools.enter_context(tc.tile_pool(name="const", bufs=1))
+        w_pool = pools.enter_context(tc.tile_pool(name="w_raw", bufs=4))
+        grouped_pool = pools.enter_context(tc.tile_pool(name="grouped", bufs=4))
+        code_pool = pools.enter_context(tc.tile_pool(name="codes", bufs=8))
+        psum_tr = pools.enter_context(tc.psum_pool(name="psum_tr", bufs=4))
+        psum_acc = pools.enter_context(tc.psum_pool(name="psum_acc", bufs=4))
+
+        ident_f32 = const.tile([P, P], F32)
+        make_identity(nc, ident_f32[:])
+        ident_bf16 = const.tile([P, P], BF16)
+        make_identity(nc, ident_bf16[:])
+
+        bias_bc = const.tile([P, 3 * E], BF16)
+        x_codes = const.tile([P, PASSES, TOKENS], U32, align_bytes=64)
+        x_scales = const.tile([P, PASSES, TOKENS], U8, align_bytes=64)
+
+        pos = const.tile([P, 1], F32)
+        for first in range(0, P, POSITIONS):
+            nc.gpsimd.iota(
+                pos[first : first + POSITIONS, :],
+                pattern=[[0, 1]],
+                base=0,
+                channel_multiplier=1,
+                allow_small_or_imprecise_dtypes=True,
+            )
+        pos_turns = const.tile([P, 1], F32)
+        nc.gpsimd.tensor_scalar(
+            out=pos_turns[:], in0=pos[:], scalar1=1.0 / (2.0 * math.pi), scalar2=0.0,
+            op0=ALU.mult, op1=ALU.add,
+        )
+        freq = const.tile([P, HALF_E], F32)
+        nc.gpsimd.memset(freq[:, 0:1], 1.0)
+        n = 1
+        while n < HALF_E:
+            nc.gpsimd.tensor_scalar(
+                out=freq[:, n : 2 * n], in0=freq[:, 0:n], scalar1=FREQ_RATIO**n, scalar2=0.0,
+                op0=ALU.mult, op1=ALU.add,
+            )
+            n *= 2
+        phase = const.tile([P, 2, HALF_E], F32)
+        for h, quarter in enumerate((0.0, 0.25)):
+            nc.gpsimd.tensor_scalar(
+                out=phase[:, h, :], in0=freq[:], scalar1=pos_turns[:, 0:1], scalar2=quarter,
+                op0=ALU.mult, op1=ALU.add,
+            )
+        whole = const.tile([P, 2, HALF_E], F32)
+        nc.gpsimd.tensor_scalar(
+            out=whole[:], in0=phase[:], scalar1=1.0, scalar2=ROUND, op0=ALU.mult, op1=ALU.add
+        )
+        nc.gpsimd.tensor_scalar(
+            out=whole[:], in0=whole[:], scalar1=-ROUND, scalar2=1.0, op0=ALU.add, op1=ALU.mult
+        )
+        nc.gpsimd.tensor_tensor(out=phase[:], in0=phase[:], in1=whole[:], op=ALU.subtract)
+        cos_t = const.tile([P, E], F32)
+        sin_t = const.tile([P, E], F32)
+        nc.scalar.activation(
+            out=cos_t[:], in_=phase[:].rearrange("p h i -> p (h i)"), func=ACT.Sin,
+            scale=2.0 * math.pi,
+        )
+        nc.scalar.activation(
+            out=sin_t[:, 0:HALF_E], in_=cos_t[:, 0:HALF_E], func=ACT.Sin, scale=-1.0
+        )
+        nc.scalar.activation(out=sin_t[:, HALF_E:E], in_=cos_t[:, HALF_E:E], func=ACT.Sin)
+        nc.scalar.activation(out=cos_t[:], in_=cos_t[:], func=ACT.Sin, bias=math.pi / 2.0)
+
+        with tc.tile_pool(name="head", bufs=1) as head:
+            x_raw = []
+            for m in range(TOKEN_TILES):
+                x_tile = head.tile([P, D], BF16, name="x_raw%d" % m)
+                nc.sync.dma_start(out=x_tile[:], in_=x_rows[m * P : (m + 1) * P, :])
+                x_raw.append(x_tile)
+            gain_bc = head.tile([P, D], BF16)
+            nc.scalar.dma_start(out=gain_bc[:], in_=g1.partition_broadcast(P))
+            shift_bc = head.tile([P, D], BF16)
+            nc.scalar.dma_start(out=shift_bc[:], in_=be1.partition_broadcast(P))
+            nc.scalar.dma_start(out=bias_bc[:], in_=bqkv.partition_broadcast(P))
+
+            xn = []
+            for m in range(TOKEN_TILES):
+                stats = head.tile([P, D // 512, 6], F32, name="stats%d" % m)
+                for j in range(D // 512):
+                    nc.vector.bn_stats(out=stats[:, j, :], in_=x_raw[m][:, j * 512 : (j + 1) * 512])
+                mean_var = head.tile([P, 2], F32, name="mean_var%d" % m)
+                nc.vector.bn_aggr(out=mean_var[:], in_=stats[:].rearrange("p c s -> p (c s)"))
+                std = head.tile([P, 1], F32, name="std%d" % m)
+                nc.scalar.activation(out=std[:], in_=mean_var[:, 1:2], func=ACT.Sqrt, bias=EPS)
+                rstd = head.tile([P, 1], F32, name="rstd%d" % m)
+                nc.vector.reciprocal(out=rstd[:], in_=std[:])
+                centred = head.tile([P, D], F32, name="centred%d" % m)
+                nc.vector.scalar_tensor_tensor(
+                    out=centred[:], in0=x_raw[m][:], scalar=mean_var[:, 0:1], in1=gain_bc[:],
+                    op0=ALU.subtract, op1=ALU.mult,
+                )
+                xn_tile = head.tile([P, 2, D // 2], BF16, name="xn%d" % m)
+                nc.vector.scalar_tensor_tensor(
+                    out=xn_tile[:],
+                    in0=centred[:].rearrange("r (w e) -> r e w", e=2),
+                    scalar=rstd[:, 0:1],
+                    in1=shift_bc[:].rearrange("r (w e) -> r e w", e=2),
+                    op0=ALU.mult, op1=ALU.add,
+                )
+                xn.append(xn_tile)
+
+            grouped_x = head.tile([P, PASSES, TOKENS, PACK], BF16, align_bytes=64)
+            for g in range(PASSES):
+                x_t = psum_tr.tile([P, PACK, TOKENS], BF16, name="x_t", tag="tr")
+                for m in range(TOKEN_TILES):
+                    for u in range(2):
+                        for e in range(2):
+                            w0 = (2 * g + u) * P
+                            nc.tensor.transpose(
+                                x_t[:, 2 * u + e, m * P : (m + 1) * P],
+                                xn[m][:, e, w0 : w0 + P],
+                                ident_bf16[:],
+                            )
+                nc.scalar.copy(out=grouped_x[:, g, :, :], in_=x_t[:].rearrange("p t r -> p r t"))
+                nc.vector.quantize_mx(
+                    out=x_codes[:, g, :].bitcast(FP8X4),
+                    scales=x_scales[:, g, :],
+                    in_=grouped_x[:, g, :, :].rearrange("p r t -> p (r t)"),
+                )
+
+        rot = pools.enter_context(tc.tile_pool(name="rot", bufs=4))
+
+        w_raw = {}
+        w_codes = {}
+        w_scales = {}
+        acc = {}
+        q_rows = {}
+        mixed = {}
+
+        def prepare(unit):
+            c, g = divmod(unit, PASSES)
+            if g == 0:
+                w_raw[c] = w_pool.tile([P, ROW_TILES, D], BF16, name="w_raw")
+                nc.sync.dma_start(
+                    out=w_raw[c][:],
+                    in_=Wqkv[c * CHUNK : (c + 1) * CHUNK, :].rearrange("(p t) k -> p t k", t=ROW_TILES),
+                )
+            grouped = grouped_pool.tile([P, CHUNK * PACK], BF16, name="grouped", align_bytes=64)
+            grouped_words = grouped[:].bitcast(F32).rearrange("p (n u) -> p n u", u=2)
+            for h in range(2):
+                w_t = psum_tr.tile([P, 2, 2 * P], F32, name="w_t", tag="tr")
+                for t2 in range(2):
+                    words = w_raw[c][:, 2 * h + t2, :].bitcast(F32)
+                    for u in range(2):
+                        w0 = g * WORDS_PER_PASS + u * P
+                        nc.tensor.transpose(
+                            w_t[:, u, t2 * P : (t2 + 1) * P], words[:, w0 : w0 + P], ident_f32[:]
+                        )
+                nc.scalar.copy(
+                    out=grouped_words[:, h * 2 * P : (h + 1) * 2 * P, :],
+                    in_=w_t[:].rearrange("p u n -> p n u"),
+                )
+            w_codes[unit] = code_pool.tile([P, CHUNK], U32, name="w_codes", align_bytes=64)
+            w_scales[unit] = code_pool.tile([P, CHUNK], U8, name="w_scales", align_bytes=64)
+            nc.vector.quantize_mx(
+                out=w_codes[unit][:].bitcast(FP8X4), scales=w_scales[unit][:], in_=grouped[:]
+            )
+
+        def multiply(unit):
+            c, g = divmod(unit, PASSES)
+            for m in range(TOKEN_TILES):
+                if g == 0:
+                    acc[m] = psum_acc.tile([P, CHUNK], F32, name="acc", tag="acc")
+                nc.tensor.matmul_mx(
+                    out=acc[m][:],
+                    lhsT=x_codes[:, g, m * P : (m + 1) * P].bitcast(FP8X4),
+                    lhsT_scale=x_scales[:, g, m * P : (m + 1) * P],
+                    rhs=w_codes[unit][:].bitcast(FP8X4),
+                    rhs_scale=w_scales[unit][:],
+                    start=(g == 0),
+                    stop=(g == PASSES - 1),
+                )
+            if g == PASSES - 1:
+                finish(c)
+
+        def add_bias(c, m, dest):
+            nc.vector.tensor_tensor(
+                out=dest.rearrange("r (p t) -> r p t", t=ROW_TILES),
+                in0=acc[m][:].rearrange("r (t p) -> r p t", t=ROW_TILES),
+                in1=bias_bc[:, c * CHUNK : (c + 1) * CHUNK].rearrange("r (p t) -> r p t", t=ROW_TILES),
+                op=ALU.add,
+            )
+
+        def finish(c):
+            which, cc = divmod(c, CHUNKS_PER_OUTPUT)
+            for m in range(TOKEN_TILES):
+                rows = out_rows[which][m * P : (m + 1) * P, :]
+                if which == 2:
+                    v_rows = rot.tile([P, CHUNK], F32, name="v_rows")
+                    add_bias(c, m, v_rows[:])
+                    nc.sync.dma_start(out=rows[:, cc * CHUNK : (cc + 1) * CHUNK], in_=v_rows[:])
+                    continue
+                if cc == 0:
+                    q_rows[m] = rot.tile([P, E], F32, name="q_rows")
+                    mixed[m] = rot.tile([P, E], F32, name="mixed")
+                q = q_rows[m]
+                add_bias(c, m, q[:, cc * CHUNK : (cc + 1) * CHUNK])
+                if cc % 2 == 1:
+                    j = cc // 2
+                    span = slice(j * HALF_E, (j + 1) * HALF_E)
+                    nc.vector.tensor_tensor(
+                        out=mixed[m][:].rearrange("r (h j i) -> r h j i", h=2, j=2)[:, :, j, :],
+                        in0=q[:, span].rearrange("r (i h) -> r h i", h=2),
+                        in1=sin_t[:].rearrange("r (h j i) -> r h j i", h=2, j=2)[:, :, j, :],
+                        op=ALU.mult,
+                    )
+                    nc.vector.tensor_tensor(out=q[:, span], in0=q[:, span], in1=cos_t[:, span], op=ALU.mult)
+                if cc == CHUNKS_PER_OUTPUT - 1:
+                    for j in range(2):
+                        span = slice(j * HALF_E, (j + 1) * HALF_E)
+                        nc.vector.tensor_tensor(
+                            out=q[:, span], in0=q[:, span], in1=mixed[m][:, span],
+                            op=(ALU.add if which == 0 else ALU.subtract),
+                        )
+                        nc.gpsimd.dma_start(out=rows[:, span], in_=q[:, span])
+
+        for first in range(0, UNITS + UNITS_PER_RUN, UNITS_PER_RUN):
+            for unit in range(first, first + UNITS_PER_RUN):
+                if unit < UNITS:
+                    prepare(unit)
+            for unit in range(first - UNITS_PER_RUN, first):
+                if unit >= 0:
+                    multiply(unit)

@@ -32,6 +32,8 @@ CHUNKS = 3 * E // CHUNK
 CHUNKS_PER_OUTPUT = E // CHUNK
 UNITS = CHUNKS * PASSES
 UNITS_PER_RUN = 2
+GAIN_ROW = CHUNKS
+SHIFT_ROW = GAIN_ROW + D // CHUNK
 
 ROUND = 1.5 * 2.0**23
 FREQ_RATIO = 10000.0 ** (-1.0 / HALF_E)
@@ -51,6 +53,7 @@ def tile_rotaryembeddingtransformerlayer_pa_kernel(
         w_pool = pools.enter_context(tc.tile_pool(name="w_raw", bufs=4))
         grouped_pool = pools.enter_context(tc.tile_pool(name="grouped", bufs=4))
         code_pool = pools.enter_context(tc.tile_pool(name="codes", bufs=8))
+        bias_pool = pools.enter_context(tc.tile_pool(name="bias", bufs=3))
         psum_tr = pools.enter_context(tc.psum_pool(name="psum_tr", bufs=4))
         psum_acc = pools.enter_context(tc.psum_pool(name="psum_acc", bufs=4))
 
@@ -59,7 +62,27 @@ def tile_rotaryembeddingtransformerlayer_pa_kernel(
         ident_bf16 = const.tile([P, P], BF16)
         make_identity(nc, ident_bf16[:])
 
-        bias_bc = const.tile([P, 3 * E], BF16)
+        vec_rows = const.tile([P, CHUNK], BF16)
+        nc.vector.memset(vec_rows[:], 0.0)
+        nc.scalar.dma_start(
+            out=vec_rows[GAIN_ROW : GAIN_ROW + D // CHUNK, :], in_=g1.rearrange("(r n) -> r n", n=CHUNK)
+        )
+        nc.scalar.dma_start(
+            out=vec_rows[SHIFT_ROW : SHIFT_ROW + D // CHUNK, :], in_=be1.rearrange("(r n) -> r n", n=CHUNK)
+        )
+        nc.scalar.dma_start(out=vec_rows[0:CHUNKS, :], in_=bqkv.rearrange("(r n) -> r n", n=CHUNK))
+
+        def broadcast_row(row, dest):
+            row_ps = psum_tr.tile([P, CHUNK], F32, name="row_ps", tag="tr")
+            nc.tensor.matmul(
+                out=row_ps[:],
+                lhsT=ident_bf16[:, row : row + 1].to_broadcast([P, P]),
+                rhs=vec_rows[:],
+                start=True,
+                stop=True,
+            )
+            nc.scalar.copy(out=dest, in_=row_ps[:])
+
         x_codes = const.tile([P, PASSES, TOKENS], U32, align_bytes=64)
         x_scales = const.tile([P, PASSES, TOKENS], U8, align_bytes=64)
 
@@ -119,10 +142,11 @@ def tile_rotaryembeddingtransformerlayer_pa_kernel(
                 nc.sync.dma_start(out=x_tile[:], in_=x_rows[m * P : (m + 1) * P, :])
                 x_raw.append(x_tile)
             gain_bc = head.tile([P, D], BF16)
-            nc.scalar.dma_start(out=gain_bc[:], in_=g1.partition_broadcast(P))
             shift_bc = head.tile([P, D], BF16)
-            nc.scalar.dma_start(out=shift_bc[:], in_=be1.partition_broadcast(P))
-            nc.scalar.dma_start(out=bias_bc[:], in_=bqkv.partition_broadcast(P))
+            for j in range(D // CHUNK):
+                broadcast_row(GAIN_ROW + j, gain_bc[:, j * CHUNK : (j + 1) * CHUNK])
+            for j in range(D // CHUNK):
+                broadcast_row(SHIFT_ROW + j, shift_bc[:, j * CHUNK : (j + 1) * CHUNK])
 
             xn = []
             for m in range(TOKEN_TILES):
@@ -175,6 +199,7 @@ def tile_rotaryembeddingtransformerlayer_pa_kernel(
         w_codes = {}
         w_scales = {}
         acc = {}
+        bias_bc = {}
         q_rows = {}
         mixed = {}
 
@@ -186,6 +211,8 @@ def tile_rotaryembeddingtransformerlayer_pa_kernel(
                     out=w_raw[c][:],
                     in_=Wqkv[c * CHUNK : (c + 1) * CHUNK, :].rearrange("(p t) k -> p t k", t=ROW_TILES),
                 )
+                bias_bc[c] = bias_pool.tile([P, CHUNK], BF16, name="bias_bc")
+                broadcast_row(c, bias_bc[c][:])
             grouped = grouped_pool.tile([P, CHUNK * PACK], BF16, name="grouped", align_bytes=64)
             grouped_words = grouped[:].bitcast(F32).rearrange("p (n u) -> p n u", u=2)
             for h in range(2):
@@ -228,7 +255,7 @@ def tile_rotaryembeddingtransformerlayer_pa_kernel(
             nc.vector.tensor_tensor(
                 out=dest.rearrange("r (p t) -> r p t", t=ROW_TILES),
                 in0=acc[m][:].rearrange("r (t p) -> r p t", t=ROW_TILES),
-                in1=bias_bc[:, c * CHUNK : (c + 1) * CHUNK].rearrange("r (p t) -> r p t", t=ROW_TILES),
+                in1=bias_bc[c][:].rearrange("r (p t) -> r p t", t=ROW_TILES),
                 op=ALU.add,
             )
 

@@ -32,6 +32,8 @@ CHUNKS = 3 * E // CHUNK
 CHUNKS_PER_OUTPUT = E // CHUNK
 UNITS = CHUNKS * PASSES
 UNITS_PER_RUN = 2
+UNITS_AHEAD = 8
+W_BUFS = 4
 GAIN_ROW = CHUNKS
 SHIFT_ROW = GAIN_ROW + D // CHUNK
 
@@ -49,28 +51,44 @@ def tile_rotaryembeddingtransformerlayer_pa_kernel(
     out_rows = [out_q.flatten_outer_dims(), out_k.flatten_outer_dims(), out_v.flatten_outer_dims()]
 
     with ExitStack() as pools:
+        pools.enter_context(tc.manual_schedule())
         const = pools.enter_context(tc.tile_pool(name="const", bufs=1))
-        w_pool = pools.enter_context(tc.tile_pool(name="w_raw", bufs=4))
-        grouped_pool = pools.enter_context(tc.tile_pool(name="grouped", bufs=4))
-        code_pool = pools.enter_context(tc.tile_pool(name="codes", bufs=8))
-        bias_pool = pools.enter_context(tc.tile_pool(name="bias", bufs=3))
+        w_pool = pools.enter_context(tc.tile_pool(name="w_raw", bufs=W_BUFS))
+        grouped_pool = pools.enter_context(tc.tile_pool(name="grouped", bufs=UNITS_AHEAD))
+        code_pool = pools.enter_context(tc.tile_pool(name="codes", bufs=UNITS_AHEAD + 4))
+        bias_pool = pools.enter_context(tc.tile_pool(name="bias", bufs=5))
         psum_tr = pools.enter_context(tc.psum_pool(name="psum_tr", bufs=4))
         psum_acc = pools.enter_context(tc.psum_pool(name="psum_acc", bufs=4))
 
-        ident_f32 = const.tile([P, P], F32)
-        make_identity(nc, ident_f32[:])
+        w_raw = {}
+        w_codes = {}
+        w_scales = {}
+        acc = {}
+        bias_bc = {}
+        q_rows = {}
+        mixed = {}
+
+        def load_chunk(c):
+            w_raw[c] = w_pool.tile([P, ROW_TILES, D], BF16, name="w_raw")
+            nc.sync.dma_start(
+                out=w_raw[c][:],
+                in_=Wqkv[c * CHUNK : (c + 1) * CHUNK, :].rearrange("(p t) k -> p t k", t=ROW_TILES),
+            )
+
         ident_bf16 = const.tile([P, P], BF16)
         make_identity(nc, ident_bf16[:])
+        ident_f32 = const.tile([P, P], F32)
+        make_identity(nc, ident_f32[:])
 
         vec_rows = const.tile([P, CHUNK], BF16)
         nc.vector.memset(vec_rows[:], 0.0)
-        nc.scalar.dma_start(
+        nc.sync.dma_start(
             out=vec_rows[GAIN_ROW : GAIN_ROW + D // CHUNK, :], in_=g1.rearrange("(r n) -> r n", n=CHUNK)
         )
-        nc.scalar.dma_start(
+        nc.sync.dma_start(
             out=vec_rows[SHIFT_ROW : SHIFT_ROW + D // CHUNK, :], in_=be1.rearrange("(r n) -> r n", n=CHUNK)
         )
-        nc.scalar.dma_start(out=vec_rows[0:CHUNKS, :], in_=bqkv.rearrange("(r n) -> r n", n=CHUNK))
+        nc.sync.dma_start(out=vec_rows[0:CHUNKS, :], in_=bqkv.rearrange("(r n) -> r n", n=CHUNK))
 
         def broadcast_row(row, dest):
             row_ps = psum_tr.tile([P, CHUNK], F32, name="row_ps", tag="tr")
@@ -85,132 +103,12 @@ def tile_rotaryembeddingtransformerlayer_pa_kernel(
 
         x_codes = const.tile([P, PASSES, TOKENS], U32, align_bytes=64)
         x_scales = const.tile([P, PASSES, TOKENS], U8, align_bytes=64)
-
-        pos = const.tile([P, 1], F32)
-        for first in range(0, P, POSITIONS):
-            nc.gpsimd.iota(
-                pos[first : first + POSITIONS, :],
-                pattern=[[0, 1]],
-                base=0,
-                channel_multiplier=1,
-                allow_small_or_imprecise_dtypes=True,
-            )
-        pos_turns = const.tile([P, 1], F32)
-        nc.gpsimd.tensor_scalar(
-            out=pos_turns[:], in0=pos[:], scalar1=1.0 / (2.0 * math.pi), scalar2=0.0,
-            op0=ALU.mult, op1=ALU.add,
-        )
-        freq = const.tile([P, HALF_E], F32)
-        nc.gpsimd.memset(freq[:, 0:1], 1.0)
-        n = 1
-        while n < HALF_E:
-            nc.gpsimd.tensor_scalar(
-                out=freq[:, n : 2 * n], in0=freq[:, 0:n], scalar1=FREQ_RATIO**n, scalar2=0.0,
-                op0=ALU.mult, op1=ALU.add,
-            )
-            n *= 2
-        phase = const.tile([P, 2, HALF_E], F32)
-        for h, quarter in enumerate((0.0, 0.25)):
-            nc.gpsimd.tensor_scalar(
-                out=phase[:, h, :], in0=freq[:], scalar1=pos_turns[:, 0:1], scalar2=quarter,
-                op0=ALU.mult, op1=ALU.add,
-            )
-        whole = const.tile([P, 2, HALF_E], F32)
-        nc.gpsimd.tensor_scalar(
-            out=whole[:], in0=phase[:], scalar1=1.0, scalar2=ROUND, op0=ALU.mult, op1=ALU.add
-        )
-        nc.gpsimd.tensor_scalar(
-            out=whole[:], in0=whole[:], scalar1=-ROUND, scalar2=1.0, op0=ALU.add, op1=ALU.mult
-        )
-        nc.gpsimd.tensor_tensor(out=phase[:], in0=phase[:], in1=whole[:], op=ALU.subtract)
         cos_t = const.tile([P, E], F32)
         sin_t = const.tile([P, E], F32)
-        nc.scalar.activation(
-            out=cos_t[:], in_=phase[:].rearrange("p h i -> p (h i)"), func=ACT.Sin,
-            scale=2.0 * math.pi,
-        )
-        nc.scalar.activation(
-            out=sin_t[:, 0:HALF_E], in_=cos_t[:, 0:HALF_E], func=ACT.Sin, scale=-1.0
-        )
-        nc.scalar.activation(out=sin_t[:, HALF_E:E], in_=cos_t[:, HALF_E:E], func=ACT.Sin)
-        nc.scalar.activation(out=cos_t[:], in_=cos_t[:], func=ACT.Sin, bias=math.pi / 2.0)
-
-        with tc.tile_pool(name="head", bufs=1) as head:
-            x_raw = []
-            for m in range(TOKEN_TILES):
-                x_tile = head.tile([P, D], BF16, name="x_raw%d" % m)
-                nc.sync.dma_start(out=x_tile[:], in_=x_rows[m * P : (m + 1) * P, :])
-                x_raw.append(x_tile)
-            gain_bc = head.tile([P, D], BF16)
-            shift_bc = head.tile([P, D], BF16)
-            for j in range(D // CHUNK):
-                broadcast_row(GAIN_ROW + j, gain_bc[:, j * CHUNK : (j + 1) * CHUNK])
-            for j in range(D // CHUNK):
-                broadcast_row(SHIFT_ROW + j, shift_bc[:, j * CHUNK : (j + 1) * CHUNK])
-
-            xn = []
-            for m in range(TOKEN_TILES):
-                stats = head.tile([P, D // 512, 6], F32, name="stats%d" % m)
-                for j in range(D // 512):
-                    nc.vector.bn_stats(out=stats[:, j, :], in_=x_raw[m][:, j * 512 : (j + 1) * 512])
-                mean_var = head.tile([P, 2], F32, name="mean_var%d" % m)
-                nc.vector.bn_aggr(out=mean_var[:], in_=stats[:].rearrange("p c s -> p (c s)"))
-                std = head.tile([P, 1], F32, name="std%d" % m)
-                nc.scalar.activation(out=std[:], in_=mean_var[:, 1:2], func=ACT.Sqrt, bias=EPS)
-                rstd = head.tile([P, 1], F32, name="rstd%d" % m)
-                nc.vector.reciprocal(out=rstd[:], in_=std[:])
-                centred = head.tile([P, D], F32, name="centred%d" % m)
-                nc.vector.scalar_tensor_tensor(
-                    out=centred[:], in0=x_raw[m][:], scalar=mean_var[:, 0:1], in1=gain_bc[:],
-                    op0=ALU.subtract, op1=ALU.mult,
-                )
-                xn_tile = head.tile([P, 2, D // 2], BF16, name="xn%d" % m)
-                nc.vector.scalar_tensor_tensor(
-                    out=xn_tile[:],
-                    in0=centred[:].rearrange("r (w e) -> r e w", e=2),
-                    scalar=rstd[:, 0:1],
-                    in1=shift_bc[:].rearrange("r (w e) -> r e w", e=2),
-                    op0=ALU.mult, op1=ALU.add,
-                )
-                xn.append(xn_tile)
-
-            grouped_x = head.tile([P, PASSES, TOKENS, PACK], BF16, align_bytes=64)
-            for g in range(PASSES):
-                x_t = psum_tr.tile([P, PACK, TOKENS], BF16, name="x_t", tag="tr")
-                for m in range(TOKEN_TILES):
-                    for u in range(2):
-                        for e in range(2):
-                            w0 = (2 * g + u) * P
-                            nc.tensor.transpose(
-                                x_t[:, 2 * u + e, m * P : (m + 1) * P],
-                                xn[m][:, e, w0 : w0 + P],
-                                ident_bf16[:],
-                            )
-                nc.scalar.copy(out=grouped_x[:, g, :, :], in_=x_t[:].rearrange("p t r -> p r t"))
-                nc.vector.quantize_mx(
-                    out=x_codes[:, g, :].bitcast(FP8X4),
-                    scales=x_scales[:, g, :],
-                    in_=grouped_x[:, g, :, :].rearrange("p r t -> p (r t)"),
-                )
-
-        rot = pools.enter_context(tc.tile_pool(name="rot", bufs=4))
-
-        w_raw = {}
-        w_codes = {}
-        w_scales = {}
-        acc = {}
-        bias_bc = {}
-        q_rows = {}
-        mixed = {}
 
         def prepare(unit):
             c, g = divmod(unit, PASSES)
             if g == 0:
-                w_raw[c] = w_pool.tile([P, ROW_TILES, D], BF16, name="w_raw")
-                nc.sync.dma_start(
-                    out=w_raw[c][:],
-                    in_=Wqkv[c * CHUNK : (c + 1) * CHUNK, :].rearrange("(p t) k -> p t k", t=ROW_TILES),
-                )
                 bias_bc[c] = bias_pool.tile([P, CHUNK], BF16, name="bias_bc")
                 broadcast_row(c, bias_bc[c][:])
             grouped = grouped_pool.tile([P, CHUNK * PACK], BF16, name="grouped", align_bytes=64)
@@ -233,23 +131,123 @@ def tile_rotaryembeddingtransformerlayer_pa_kernel(
             nc.vector.quantize_mx(
                 out=w_codes[unit][:].bitcast(FP8X4), scales=w_scales[unit][:], in_=grouped[:]
             )
+            if g == PASSES - 1 and c + W_BUFS < CHUNKS:
+                load_chunk(c + W_BUFS)
 
-        def multiply(unit):
-            c, g = divmod(unit, PASSES)
+        with tc.tile_pool(name="head", bufs=1) as head:
+            x_raw = []
             for m in range(TOKEN_TILES):
-                if g == 0:
-                    acc[m] = psum_acc.tile([P, CHUNK], F32, name="acc", tag="acc")
-                nc.tensor.matmul_mx(
-                    out=acc[m][:],
-                    lhsT=x_codes[:, g, m * P : (m + 1) * P].bitcast(FP8X4),
-                    lhsT_scale=x_scales[:, g, m * P : (m + 1) * P],
-                    rhs=w_codes[unit][:].bitcast(FP8X4),
-                    rhs_scale=w_scales[unit][:],
-                    start=(g == 0),
-                    stop=(g == PASSES - 1),
+                x_tile = head.tile([P, D], BF16, name="x_raw%d" % m)
+                nc.sync.dma_start(out=x_tile[:], in_=x_rows[m * P : (m + 1) * P, :])
+                x_raw.append(x_tile)
+            for c in range(W_BUFS):
+                load_chunk(c)
+
+            pos = head.tile([P, 1], F32)
+            for first in range(0, P, POSITIONS):
+                nc.gpsimd.iota(
+                    pos[first : first + POSITIONS, :],
+                    pattern=[[0, 1]],
+                    base=0,
+                    channel_multiplier=1,
+                    allow_small_or_imprecise_dtypes=True,
                 )
-            if g == PASSES - 1:
-                finish(c)
+            pos_turns = head.tile([P, 1], F32)
+            nc.gpsimd.tensor_scalar(
+                out=pos_turns[:], in0=pos[:], scalar1=1.0 / (2.0 * math.pi), scalar2=0.0,
+                op0=ALU.mult, op1=ALU.add,
+            )
+            freq = head.tile([P, HALF_E], F32)
+            nc.gpsimd.memset(freq[:, 0:1], 1.0)
+            n = 1
+            while n < HALF_E:
+                nc.gpsimd.tensor_scalar(
+                    out=freq[:, n : 2 * n], in0=freq[:, 0:n], scalar1=FREQ_RATIO**n, scalar2=0.0,
+                    op0=ALU.mult, op1=ALU.add,
+                )
+                n *= 2
+            phase = head.tile([P, 2, HALF_E], F32)
+            for h, quarter in enumerate((0.0, 0.25)):
+                nc.gpsimd.tensor_scalar(
+                    out=phase[:, h, :], in0=freq[:], scalar1=pos_turns[:, 0:1], scalar2=quarter,
+                    op0=ALU.mult, op1=ALU.add,
+                )
+            whole = head.tile([P, 2, HALF_E], F32)
+            nc.gpsimd.tensor_scalar(
+                out=whole[:], in0=phase[:], scalar1=1.0, scalar2=ROUND, op0=ALU.mult, op1=ALU.add
+            )
+            nc.gpsimd.tensor_scalar(
+                out=whole[:], in0=whole[:], scalar1=-ROUND, scalar2=1.0, op0=ALU.add, op1=ALU.mult
+            )
+            nc.gpsimd.tensor_tensor(out=phase[:], in0=phase[:], in1=whole[:], op=ALU.subtract)
+
+            gain_bc = head.tile([P, D], BF16)
+            shift_bc = head.tile([P, D], BF16)
+            mean_var = []
+            std = []
+            for m, (first_row, spread) in enumerate(((GAIN_ROW, gain_bc), (SHIFT_ROW, shift_bc))):
+                for j in range(D // CHUNK):
+                    broadcast_row(first_row + j, spread[:, j * CHUNK : (j + 1) * CHUNK])
+                stats = head.tile([P, D // 512, 6], F32, name="stats%d" % m)
+                for j in range(D // 512):
+                    nc.vector.bn_stats(out=stats[:, j, :], in_=x_raw[m][:, j * 512 : (j + 1) * 512])
+                mean_var.append(head.tile([P, 2], F32, name="mean_var%d" % m))
+                nc.vector.bn_aggr(out=mean_var[m][:], in_=stats[:].rearrange("p c s -> p (c s)"))
+                std.append(head.tile([P, 1], F32, name="std%d" % m))
+                nc.scalar.activation(out=std[m][:], in_=mean_var[m][:, 1:2], func=ACT.Sqrt, bias=EPS)
+            xn = []
+            for m in range(TOKEN_TILES):
+                rstd = head.tile([P, 1], F32, name="rstd%d" % m)
+                nc.vector.reciprocal(out=rstd[:], in_=std[m][:])
+                centred = head.tile([P, D], F32, name="centred%d" % m)
+                nc.vector.scalar_tensor_tensor(
+                    out=centred[:], in0=x_raw[m][:], scalar=mean_var[m][:, 0:1], in1=gain_bc[:],
+                    op0=ALU.subtract, op1=ALU.mult,
+                )
+                xn_tile = head.tile([P, 2, D // 2], BF16, name="xn%d" % m)
+                nc.vector.scalar_tensor_tensor(
+                    out=xn_tile[:],
+                    in0=centred[:].rearrange("r (w e) -> r e w", e=2),
+                    scalar=rstd[:, 0:1],
+                    in1=shift_bc[:].rearrange("r (w e) -> r e w", e=2),
+                    op0=ALU.mult, op1=ALU.add,
+                )
+                xn.append(xn_tile)
+
+            for unit in range(UNITS_AHEAD):
+                prepare(unit)
+
+            grouped_x = head.tile([P, PASSES, TOKENS, PACK], BF16, align_bytes=64)
+            for g in range(PASSES):
+                x_t = psum_tr.tile([P, PACK, TOKENS], BF16, name="x_t", tag="tr")
+                for m in range(TOKEN_TILES):
+                    for u in range(2):
+                        for e in range(2):
+                            w0 = (2 * g + u) * P
+                            nc.tensor.transpose(
+                                x_t[:, 2 * u + e, m * P : (m + 1) * P],
+                                xn[m][:, e, w0 : w0 + P],
+                                ident_bf16[:],
+                            )
+                nc.scalar.copy(out=grouped_x[:, g, :, :], in_=x_t[:].rearrange("p t r -> p r t"))
+            for g in range(PASSES):
+                nc.vector.quantize_mx(
+                    out=x_codes[:, g, :].bitcast(FP8X4),
+                    scales=x_scales[:, g, :],
+                    in_=grouped_x[:, g, :, :].rearrange("p r t -> p (r t)"),
+                )
+
+            nc.scalar.activation(
+                out=cos_t[:], in_=phase[:].rearrange("p h i -> p (h i)"), func=ACT.Sin,
+                scale=2.0 * math.pi,
+            )
+            nc.scalar.activation(
+                out=sin_t[:, 0:HALF_E], in_=cos_t[:, 0:HALF_E], func=ACT.Sin, scale=-1.0
+            )
+            nc.scalar.activation(out=sin_t[:, HALF_E:E], in_=cos_t[:, HALF_E:E], func=ACT.Sin)
+            nc.scalar.activation(out=cos_t[:], in_=cos_t[:], func=ACT.Sin, bias=math.pi / 2.0)
+
+        rot = pools.enter_context(tc.tile_pool(name="rot", bufs=4))
 
         def add_bias(c, m, dest):
             nc.vector.tensor_tensor(
@@ -292,10 +290,26 @@ def tile_rotaryembeddingtransformerlayer_pa_kernel(
                         )
                         nc.gpsimd.dma_start(out=rows[:, span], in_=q[:, span])
 
-        for first in range(0, UNITS + UNITS_PER_RUN, UNITS_PER_RUN):
+        def multiply(unit):
+            c, g = divmod(unit, PASSES)
+            for m in range(TOKEN_TILES):
+                if g == 0:
+                    acc[m] = psum_acc.tile([P, CHUNK], F32, name="acc", tag="acc")
+                nc.tensor.matmul_mx(
+                    out=acc[m][:],
+                    lhsT=x_codes[:, g, m * P : (m + 1) * P].bitcast(FP8X4),
+                    lhsT_scale=x_scales[:, g, m * P : (m + 1) * P],
+                    rhs=w_codes[unit][:].bitcast(FP8X4),
+                    rhs_scale=w_scales[unit][:],
+                    start=(g == 0),
+                    stop=(g == PASSES - 1),
+                )
+            if g == PASSES - 1:
+                finish(c)
+
+        for first in range(UNITS_AHEAD, UNITS + UNITS_AHEAD, UNITS_PER_RUN):
+            for unit in range(first - UNITS_AHEAD, first - UNITS_AHEAD + UNITS_PER_RUN):
+                multiply(unit)
             for unit in range(first, first + UNITS_PER_RUN):
                 if unit < UNITS:
                     prepare(unit)
-            for unit in range(first - UNITS_PER_RUN, first):
-                if unit >= 0:
-                    multiply(unit)

@@ -31,7 +31,7 @@ ROW_TILES = CHUNK // P
 CHUNKS = 3 * E // CHUNK
 CHUNKS_PER_OUTPUT = E // CHUNK
 UNITS = CHUNKS * PASSES
-UNITS_PER_RUN = 2
+UNITS_PER_RUN = 1
 UNITS_AHEAD = 8
 W_BUFS = 4
 GAIN_ROW = CHUNKS

@@ -30,15 +30,16 @@ CHUNK = 512
 ROW_TILES = CHUNK // P
 CHUNKS = 3 * E // CHUNK
 CHUNKS_PER_OUTPUT = E // CHUNK
-UNITS = CHUNKS * PASSES
-UNITS_PER_RUN = 1
-UNITS_AHEAD = 8
+SLAB_PASSES = 2
+SLABS_PER_CHUNK = PASSES // SLAB_PASSES
+SLABS = CHUNKS * SLABS_PER_CHUNK
+SLABS_AHEAD = 4
+SLABS_BEFORE_X = 2
 W_BUFS = 4
-GAIN_ROW = CHUNKS
-SHIFT_ROW = GAIN_ROW + D // CHUNK
 
 ROUND = 1.5 * 2.0**23
 FREQ_RATIO = 10000.0 ** (-1.0 / HALF_E)
+REDUCED = HALF_E // 2
 
 FLOPS = 2 * TOKENS * D * 3 * E
 
@@ -54,19 +55,23 @@ def tile_rotaryembeddingtransformerlayer_pa_kernel(
         pools.enter_context(tc.manual_schedule())
         const = pools.enter_context(tc.tile_pool(name="const", bufs=1))
         w_pool = pools.enter_context(tc.tile_pool(name="w_raw", bufs=W_BUFS))
-        grouped_pool = pools.enter_context(tc.tile_pool(name="grouped", bufs=UNITS_AHEAD))
-        code_pool = pools.enter_context(tc.tile_pool(name="codes", bufs=UNITS_AHEAD + 4))
-        bias_pool = pools.enter_context(tc.tile_pool(name="bias", bufs=5))
+        grouped_pool = pools.enter_context(tc.tile_pool(name="grouped", bufs=SLABS_AHEAD))
+        code_pool = pools.enter_context(tc.tile_pool(name="codes", bufs=SLABS_AHEAD + 2))
         psum_tr = pools.enter_context(tc.psum_pool(name="psum_tr", bufs=4))
         psum_acc = pools.enter_context(tc.psum_pool(name="psum_acc", bufs=4))
+
+        ident = const.tile([P, P], F32)
+        bias_bc = const.tile([P, 3 * E], BF16)
+        x_codes = const.tile([P, PASSES * TOKENS], U32, align_bytes=64)
+        x_scales = const.tile([P, PASSES * TOKENS], U8, align_bytes=64)
+        cos_t = const.tile([P, E], F32)
+        sin_t = const.tile([P, E], F32)
 
         w_raw = {}
         w_codes = {}
         w_scales = {}
         acc = {}
-        bias_bc = {}
         q_rows = {}
-        mixed = {}
 
         def load_chunk(c):
             w_raw[c] = w_pool.tile([P, ROW_TILES, D], BF16, name="w_raw")
@@ -74,72 +79,50 @@ def tile_rotaryembeddingtransformerlayer_pa_kernel(
                 out=w_raw[c][:],
                 in_=Wqkv[c * CHUNK : (c + 1) * CHUNK, :].rearrange("(p t) k -> p t k", t=ROW_TILES),
             )
+            if c % CHUNKS_PER_OUTPUT == 0:
+                span = slice(c * CHUNK, c * CHUNK + E)
+                nc.sync.dma_start(out=bias_bc[:, span], in_=bqkv[span].partition_broadcast(P))
 
-        ident_bf16 = const.tile([P, P], BF16)
-        make_identity(nc, ident_bf16[:])
-        ident_f32 = const.tile([P, P], F32)
-        make_identity(nc, ident_f32[:])
+        def transpose_words(rows_of, g, width, dest_words):
+            w_t = psum_tr.tile([P, 2, width], F32, name="w_t", tag="tr")
+            for j in range(width // P):
+                words = rows_of(j).bitcast(F32)
+                for u in range(2):
+                    w0 = g * WORDS_PER_PASS + u * P
+                    nc.tensor.transpose(w_t[:, u, j * P : (j + 1) * P], words[:, w0 : w0 + P], ident[:])
+            nc.scalar.copy(out=dest_words, in_=w_t[:].rearrange("p u n -> p n u"))
 
-        vec_rows = const.tile([P, CHUNK], BF16)
-        nc.vector.memset(vec_rows[:], 0.0)
-        nc.sync.dma_start(
-            out=vec_rows[GAIN_ROW : GAIN_ROW + D // CHUNK, :], in_=g1.rearrange("(r n) -> r n", n=CHUNK)
-        )
-        nc.sync.dma_start(
-            out=vec_rows[SHIFT_ROW : SHIFT_ROW + D // CHUNK, :], in_=be1.rearrange("(r n) -> r n", n=CHUNK)
-        )
-        nc.sync.dma_start(out=vec_rows[0:CHUNKS, :], in_=bqkv.rearrange("(r n) -> r n", n=CHUNK))
-
-        def broadcast_row(row, dest):
-            row_ps = psum_tr.tile([P, CHUNK], F32, name="row_ps", tag="tr")
-            nc.tensor.matmul(
-                out=row_ps[:],
-                lhsT=ident_bf16[:, row : row + 1].to_broadcast([P, P]),
-                rhs=vec_rows[:],
-                start=True,
-                stop=True,
+        def prepare(slab):
+            c, part = divmod(slab, SLABS_PER_CHUNK)
+            grouped = grouped_pool.tile(
+                [P, SLAB_PASSES * CHUNK * PACK], BF16, name="grouped", align_bytes=64
             )
-            nc.scalar.copy(out=dest, in_=row_ps[:])
-
-        x_codes = const.tile([P, PASSES, TOKENS], U32, align_bytes=64)
-        x_scales = const.tile([P, PASSES, TOKENS], U8, align_bytes=64)
-        cos_t = const.tile([P, E], F32)
-        sin_t = const.tile([P, E], F32)
-
-        def prepare(unit):
-            c, g = divmod(unit, PASSES)
-            if g == 0:
-                bias_bc[c] = bias_pool.tile([P, CHUNK], BF16, name="bias_bc")
-                broadcast_row(c, bias_bc[c][:])
-            grouped = grouped_pool.tile([P, CHUNK * PACK], BF16, name="grouped", align_bytes=64)
-            grouped_words = grouped[:].bitcast(F32).rearrange("p (n u) -> p n u", u=2)
-            for h in range(2):
-                w_t = psum_tr.tile([P, 2, 2 * P], F32, name="w_t", tag="tr")
-                for t2 in range(2):
-                    words = w_raw[c][:, 2 * h + t2, :].bitcast(F32)
-                    for u in range(2):
-                        w0 = g * WORDS_PER_PASS + u * P
-                        nc.tensor.transpose(
-                            w_t[:, u, t2 * P : (t2 + 1) * P], words[:, w0 : w0 + P], ident_f32[:]
-                        )
-                nc.scalar.copy(
-                    out=grouped_words[:, h * 2 * P : (h + 1) * 2 * P, :],
-                    in_=w_t[:].rearrange("p u n -> p n u"),
-                )
-            w_codes[unit] = code_pool.tile([P, CHUNK], U32, name="w_codes", align_bytes=64)
-            w_scales[unit] = code_pool.tile([P, CHUNK], U8, name="w_scales", align_bytes=64)
+            grouped_words = grouped[:].bitcast(F32).rearrange("p (i n u) -> p i n u", i=SLAB_PASSES, u=2)
+            for i in range(SLAB_PASSES):
+                for h in range(2):
+                    transpose_words(
+                        lambda j: w_raw[c][:, 2 * h + j, :],
+                        part * SLAB_PASSES + i,
+                        2 * P,
+                        grouped_words[:, i, h * 2 * P : (h + 1) * 2 * P, :],
+                    )
+            w_codes[slab] = code_pool.tile([P, SLAB_PASSES * CHUNK], U32, name="w_codes", align_bytes=64)
+            w_scales[slab] = code_pool.tile([P, SLAB_PASSES * CHUNK], U8, name="w_scales", align_bytes=64)
             nc.vector.quantize_mx(
-                out=w_codes[unit][:].bitcast(FP8X4), scales=w_scales[unit][:], in_=grouped[:]
+                out=w_codes[slab][:].bitcast(FP8X4), scales=w_scales[slab][:], in_=grouped[:]
             )
-            if g == PASSES - 1 and c + W_BUFS < CHUNKS:
+            if part == SLABS_PER_CHUNK - 1 and c + W_BUFS < CHUNKS:
                 load_chunk(c + W_BUFS)
 
         with tc.tile_pool(name="head", bufs=1) as head:
             x_raw = []
             for m in range(TOKEN_TILES):
-                x_tile = head.tile([P, D], BF16, name="x_raw%d" % m)
-                nc.sync.dma_start(out=x_tile[:], in_=x_rows[m * P : (m + 1) * P, :])
-                x_raw.append(x_tile)
+                x_raw.append(head.tile([P, D], BF16, name="x_raw%d" % m))
+                nc.sync.dma_start(out=x_raw[m][:], in_=x_rows[m * P : (m + 1) * P, :])
+            gain_bc = head.tile([P, D], BF16)
+            nc.sync.dma_start(out=gain_bc[:], in_=g1.partition_broadcast(P))
+            shift_bc = head.tile([P, D], BF16)
+            nc.sync.dma_start(out=shift_bc[:], in_=be1.partition_broadcast(P))
             for c in range(W_BUFS):
                 load_chunk(c)
 
@@ -152,100 +135,76 @@ def tile_rotaryembeddingtransformerlayer_pa_kernel(
                     channel_multiplier=1,
                     allow_small_or_imprecise_dtypes=True,
                 )
-            pos_turns = head.tile([P, 1], F32)
+            turns = head.tile([P, HALF_E], F32)
             nc.gpsimd.tensor_scalar(
-                out=pos_turns[:], in0=pos[:], scalar1=1.0 / (2.0 * math.pi), scalar2=0.0,
+                out=turns[:, 0:1], in0=pos[:], scalar1=1.0 / (2.0 * math.pi), scalar2=0.0,
                 op0=ALU.mult, op1=ALU.add,
             )
-            freq = head.tile([P, HALF_E], F32)
-            nc.gpsimd.memset(freq[:, 0:1], 1.0)
+            make_identity(nc, ident[:])
             n = 1
             while n < HALF_E:
-                nc.gpsimd.tensor_scalar(
-                    out=freq[:, n : 2 * n], in0=freq[:, 0:n], scalar1=FREQ_RATIO**n, scalar2=0.0,
-                    op0=ALU.mult, op1=ALU.add,
+                nc.vector.tensor_scalar(
+                    out=turns[:, n : 2 * n], in0=turns[:, 0:n], scalar1=FREQ_RATIO**n, scalar2=None,
+                    op0=ALU.mult,
                 )
                 n *= 2
-            phase = head.tile([P, 2, HALF_E], F32)
-            for h, quarter in enumerate((0.0, 0.25)):
-                nc.gpsimd.tensor_scalar(
-                    out=phase[:, h, :], in0=freq[:], scalar1=pos_turns[:, 0:1], scalar2=quarter,
-                    op0=ALU.mult, op1=ALU.add,
-                )
-            whole = head.tile([P, 2, HALF_E], F32)
-            nc.gpsimd.tensor_scalar(
-                out=whole[:], in0=phase[:], scalar1=1.0, scalar2=ROUND, op0=ALU.mult, op1=ALU.add
+            whole = head.tile([P, REDUCED], F32)
+            nc.vector.tensor_scalar(
+                out=whole[:], in0=turns[:, 0:REDUCED], scalar1=ROUND, scalar2=ROUND,
+                op0=ALU.add, op1=ALU.subtract,
             )
-            nc.gpsimd.tensor_scalar(
-                out=whole[:], in0=whole[:], scalar1=-ROUND, scalar2=1.0, op0=ALU.add, op1=ALU.mult
+            nc.vector.tensor_tensor(
+                out=turns[:, 0:REDUCED], in0=turns[:, 0:REDUCED], in1=whole[:], op=ALU.subtract
             )
-            nc.gpsimd.tensor_tensor(out=phase[:], in0=phase[:], in1=whole[:], op=ALU.subtract)
+            abs_turns = head.tile([P, HALF_E], F32)
+            nc.vector.scalar_tensor_tensor(
+                out=abs_turns[:], in0=turns[:], scalar=-1.0, in1=turns[:], op0=ALU.mult, op1=ALU.max
+            )
+            nc.scalar.activation(out=cos_t[:, 0:HALF_E], in_=turns[:], func=ACT.Sin, scale=2.0 * math.pi)
+            nc.scalar.activation(
+                out=cos_t[:, HALF_E:E], in_=abs_turns[:], func=ACT.Sin,
+                scale=-2.0 * math.pi, bias=math.pi / 2.0,
+            )
+            nc.scalar.activation(out=sin_t[:, 0:HALF_E], in_=cos_t[:, 0:HALF_E], func=ACT.Sin, scale=-1.0)
+            nc.scalar.activation(out=sin_t[:, HALF_E:E], in_=cos_t[:, HALF_E:E], func=ACT.Sin)
+            nc.scalar.activation(out=cos_t[:], in_=cos_t[:], func=ACT.Sin, bias=math.pi / 2.0)
 
-            gain_bc = head.tile([P, D], BF16)
-            shift_bc = head.tile([P, D], BF16)
-            mean_var = []
-            std = []
-            for m, (first_row, spread) in enumerate(((GAIN_ROW, gain_bc), (SHIFT_ROW, shift_bc))):
-                for j in range(D // CHUNK):
-                    broadcast_row(first_row + j, spread[:, j * CHUNK : (j + 1) * CHUNK])
+            mean_var = head.tile([P, TOKEN_TILES, 2], F32)
+            for m in range(TOKEN_TILES):
                 stats = head.tile([P, D // 512, 6], F32, name="stats%d" % m)
                 for j in range(D // 512):
                     nc.vector.bn_stats(out=stats[:, j, :], in_=x_raw[m][:, j * 512 : (j + 1) * 512])
-                mean_var.append(head.tile([P, 2], F32, name="mean_var%d" % m))
-                nc.vector.bn_aggr(out=mean_var[m][:], in_=stats[:].rearrange("p c s -> p (c s)"))
-                std.append(head.tile([P, 1], F32, name="std%d" % m))
-                nc.scalar.activation(out=std[m][:], in_=mean_var[m][:, 1:2], func=ACT.Sqrt, bias=EPS)
-            xn = []
+                nc.vector.bn_aggr(out=mean_var[:, m, :], in_=stats[:].rearrange("p c s -> p (c s)"))
+            std = head.tile([P, TOKEN_TILES], F32)
+            nc.scalar.activation(out=std[:], in_=mean_var[:, :, 1], func=ACT.Sqrt, bias=EPS)
+            centred = []
             for m in range(TOKEN_TILES):
-                rstd = head.tile([P, 1], F32, name="rstd%d" % m)
-                nc.vector.reciprocal(out=rstd[:], in_=std[m][:])
-                centred = head.tile([P, D], F32, name="centred%d" % m)
+                centred.append(head.tile([P, D], F32, name="centred%d" % m))
                 nc.vector.scalar_tensor_tensor(
-                    out=centred[:], in0=x_raw[m][:], scalar=mean_var[m][:, 0:1], in1=gain_bc[:],
+                    out=centred[m][:], in0=x_raw[m][:], scalar=mean_var[:, m, 0:1], in1=gain_bc[:],
                     op0=ALU.subtract, op1=ALU.mult,
                 )
-                xn_tile = head.tile([P, 2, D // 2], BF16, name="xn%d" % m)
+            rstd = head.tile([P, TOKEN_TILES], F32)
+            nc.vector.reciprocal(out=rstd[:], in_=std[:])
+            xn = []
+            for m in range(TOKEN_TILES):
+                xn.append(head.tile([P, D], BF16, name="xn%d" % m))
                 nc.vector.scalar_tensor_tensor(
-                    out=xn_tile[:],
-                    in0=centred[:].rearrange("r (w e) -> r e w", e=2),
-                    scalar=rstd[:, 0:1],
-                    in1=shift_bc[:].rearrange("r (w e) -> r e w", e=2),
+                    out=xn[m][:], in0=centred[m][:], scalar=rstd[:, m : m + 1], in1=shift_bc[:],
                     op0=ALU.mult, op1=ALU.add,
                 )
-                xn.append(xn_tile)
 
-            for unit in range(UNITS_AHEAD):
-                prepare(unit)
+            for slab in range(SLABS_BEFORE_X):
+                prepare(slab)
 
-            grouped_x = head.tile([P, PASSES, TOKENS, PACK], BF16, align_bytes=64)
+            grouped_x = head.tile([P, PASSES * TOKENS * PACK], BF16, align_bytes=64)
+            grouped_x_words = grouped_x[:].bitcast(F32).rearrange("p (g r u) -> p g r u", g=PASSES, u=2)
             for g in range(PASSES):
-                x_t = psum_tr.tile([P, PACK, TOKENS], BF16, name="x_t", tag="tr")
-                for m in range(TOKEN_TILES):
-                    for u in range(2):
-                        for e in range(2):
-                            w0 = (2 * g + u) * P
-                            nc.tensor.transpose(
-                                x_t[:, 2 * u + e, m * P : (m + 1) * P],
-                                xn[m][:, e, w0 : w0 + P],
-                                ident_bf16[:],
-                            )
-                nc.scalar.copy(out=grouped_x[:, g, :, :], in_=x_t[:].rearrange("p t r -> p r t"))
-            for g in range(PASSES):
-                nc.vector.quantize_mx(
-                    out=x_codes[:, g, :].bitcast(FP8X4),
-                    scales=x_scales[:, g, :],
-                    in_=grouped_x[:, g, :, :].rearrange("p r t -> p (r t)"),
-                )
+                transpose_words(lambda m: xn[m][:], g, TOKENS, grouped_x_words[:, g, :, :])
+            nc.vector.quantize_mx(out=x_codes[:].bitcast(FP8X4), scales=x_scales[:], in_=grouped_x[:])
 
-            nc.scalar.activation(
-                out=cos_t[:], in_=phase[:].rearrange("p h i -> p (h i)"), func=ACT.Sin,
-                scale=2.0 * math.pi,
-            )
-            nc.scalar.activation(
-                out=sin_t[:, 0:HALF_E], in_=cos_t[:, 0:HALF_E], func=ACT.Sin, scale=-1.0
-            )
-            nc.scalar.activation(out=sin_t[:, HALF_E:E], in_=cos_t[:, HALF_E:E], func=ACT.Sin)
-            nc.scalar.activation(out=cos_t[:], in_=cos_t[:], func=ACT.Sin, bias=math.pi / 2.0)
+            for slab in range(SLABS_BEFORE_X, SLABS_AHEAD):
+                prepare(slab)
 
         rot = pools.enter_context(tc.tile_pool(name="rot", bufs=4))
 
@@ -253,7 +212,7 @@ def tile_rotaryembeddingtransformerlayer_pa_kernel(
             nc.vector.tensor_tensor(
                 out=dest.rearrange("r (p t) -> r p t", t=ROW_TILES),
                 in0=acc[m][:].rearrange("r (t p) -> r p t", t=ROW_TILES),
-                in1=bias_bc[c][:].rearrange("r (p t) -> r p t", t=ROW_TILES),
+                in1=bias_bc[:, c * CHUNK : (c + 1) * CHUNK].rearrange("r (p t) -> r p t", t=ROW_TILES),
                 op=ALU.add,
             )
 
@@ -268,48 +227,43 @@ def tile_rotaryembeddingtransformerlayer_pa_kernel(
                     continue
                 if cc == 0:
                     q_rows[m] = rot.tile([P, E], F32, name="q_rows")
-                    mixed[m] = rot.tile([P, E], F32, name="mixed")
                 q = q_rows[m]
                 add_bias(c, m, q[:, cc * CHUNK : (cc + 1) * CHUNK])
-                if cc % 2 == 1:
-                    j = cc // 2
-                    span = slice(j * HALF_E, (j + 1) * HALF_E)
+                if cc == CHUNKS_PER_OUTPUT - 1:
+                    mixed = rot.tile([P, E], F32, name="mixed", bufs=2)
                     nc.vector.tensor_tensor(
-                        out=mixed[m][:].rearrange("r (h j i) -> r h j i", h=2, j=2)[:, :, j, :],
-                        in0=q[:, span].rearrange("r (i h) -> r h i", h=2),
-                        in1=sin_t[:].rearrange("r (h j i) -> r h j i", h=2, j=2)[:, :, j, :],
+                        out=mixed[:].rearrange("r (h i) -> r h i", h=2),
+                        in0=q[:].rearrange("r (i h) -> r h i", h=2),
+                        in1=sin_t[:].rearrange("r (h i) -> r h i", h=2),
                         op=ALU.mult,
                     )
-                    nc.vector.tensor_tensor(out=q[:, span], in0=q[:, span], in1=cos_t[:, span], op=ALU.mult)
-                if cc == CHUNKS_PER_OUTPUT - 1:
-                    for j in range(2):
-                        span = slice(j * HALF_E, (j + 1) * HALF_E)
-                        nc.vector.tensor_tensor(
-                            out=q[:, span], in0=q[:, span], in1=mixed[m][:, span],
-                            op=(ALU.add if which == 0 else ALU.subtract),
-                        )
-                        nc.gpsimd.dma_start(out=rows[:, span], in_=q[:, span])
+                    nc.vector.tensor_tensor(out=q[:], in0=q[:], in1=cos_t[:], op=ALU.mult)
+                    nc.vector.tensor_tensor(
+                        out=q[:], in0=q[:], in1=mixed[:], op=(ALU.add if which == 0 else ALU.subtract)
+                    )
+                    nc.gpsimd.dma_start(out=rows, in_=q[:])
 
-        def multiply(unit):
-            c, g = divmod(unit, PASSES)
-            for m in range(TOKEN_TILES):
-                if g == 0:
-                    acc[m] = psum_acc.tile([P, CHUNK], F32, name="acc", tag="acc")
-                nc.tensor.matmul_mx(
-                    out=acc[m][:],
-                    lhsT=x_codes[:, g, m * P : (m + 1) * P].bitcast(FP8X4),
-                    lhsT_scale=x_scales[:, g, m * P : (m + 1) * P],
-                    rhs=w_codes[unit][:].bitcast(FP8X4),
-                    rhs_scale=w_scales[unit][:],
-                    start=(g == 0),
-                    stop=(g == PASSES - 1),
-                )
-            if g == PASSES - 1:
+        def multiply(slab):
+            c, part = divmod(slab, SLABS_PER_CHUNK)
+            for i in range(SLAB_PASSES):
+                g = part * SLAB_PASSES + i
+                for m in range(TOKEN_TILES):
+                    if g == 0:
+                        acc[m] = psum_acc.tile([P, CHUNK], F32, name="acc", tag="acc")
+                    tokens = slice(g * TOKENS + m * P, g * TOKENS + (m + 1) * P)
+                    nc.tensor.matmul_mx(
+                        out=acc[m][:],
+                        lhsT=x_codes[:, tokens].bitcast(FP8X4),
+                        lhsT_scale=x_scales[:, tokens],
+                        rhs=w_codes[slab][:, i * CHUNK : (i + 1) * CHUNK].bitcast(FP8X4),
+                        rhs_scale=w_scales[slab][:, i * CHUNK : (i + 1) * CHUNK],
+                        start=(g == 0),
+                        stop=(g == PASSES - 1),
+                    )
+            if part == SLABS_PER_CHUNK - 1:
                 finish(c)
 
-        for first in range(UNITS_AHEAD, UNITS + UNITS_AHEAD, UNITS_PER_RUN):
-            for unit in range(first - UNITS_AHEAD, first - UNITS_AHEAD + UNITS_PER_RUN):
-                multiply(unit)
-            for unit in range(first, first + UNITS_PER_RUN):
-                if unit < UNITS:
-                    prepare(unit)
+        for slab in range(SLABS_AHEAD, SLABS + SLABS_AHEAD):
+            multiply(slab - SLABS_AHEAD)
+            if slab < SLABS:
+                prepare(slab)

@@ -72,6 +72,7 @@ def tile_rotaryembeddingtransformerlayer_pa_kernel(
         w_scales = {}
         acc = {}
         q_rows = {}
+        mixed = {}
 
         def load_chunk(c):
             w_raw[c] = w_pool.tile([P, ROW_TILES, D], BF16, name="w_raw")
@@ -216,32 +217,43 @@ def tile_rotaryembeddingtransformerlayer_pa_kernel(
                 op=ALU.add,
             )
 
-        def finish(c):
+        def finish_v(c):
+            cc = c % CHUNKS_PER_OUTPUT
+            for m in range(TOKEN_TILES):
+                v_rows = rot.tile([P, CHUNK], F32, name="v_rows")
+                add_bias(c, m, v_rows[:])
+                nc.sync.dma_start(
+                    out=out_rows[2][m * P : (m + 1) * P, cc * CHUNK : (cc + 1) * CHUNK], in_=v_rows[:]
+                )
+
+        def finish_q_or_k(c):
             which, cc = divmod(c, CHUNKS_PER_OUTPUT)
             for m in range(TOKEN_TILES):
-                rows = out_rows[which][m * P : (m + 1) * P, :]
-                if which == 2:
-                    v_rows = rot.tile([P, CHUNK], F32, name="v_rows")
-                    add_bias(c, m, v_rows[:])
-                    nc.sync.dma_start(out=rows[:, cc * CHUNK : (cc + 1) * CHUNK], in_=v_rows[:])
-                    continue
                 if cc == 0:
                     q_rows[m] = rot.tile([P, E], F32, name="q_rows")
-                q = q_rows[m]
-                add_bias(c, m, q[:, cc * CHUNK : (cc + 1) * CHUNK])
-                if cc == CHUNKS_PER_OUTPUT - 1:
-                    mixed = rot.tile([P, E], F32, name="mixed", bufs=2)
+                    mixed[m] = rot.tile([P, E], F32, name="mixed", bufs=TOKEN_TILES)
+                add_bias(c, m, q_rows[m][:, cc * CHUNK : (cc + 1) * CHUNK])
+            if cc % 2 == 1:
+                j = cc // 2
+                span = slice(j * HALF_E, (j + 1) * HALF_E)
+                for m in range(TOKEN_TILES):
                     nc.vector.tensor_tensor(
-                        out=mixed[:].rearrange("r (h i) -> r h i", h=2),
-                        in0=q[:].rearrange("r (i h) -> r h i", h=2),
-                        in1=sin_t[:].rearrange("r (h i) -> r h i", h=2),
+                        out=mixed[m][:].rearrange("r (h j i) -> r h j i", h=2, j=2)[:, :, j, :],
+                        in0=q_rows[m][:, span].rearrange("r (i h) -> r h i", h=2),
+                        in1=sin_t[:].rearrange("r (h j i) -> r h j i", h=2, j=2)[:, :, j, :],
                         op=ALU.mult,
                     )
-                    nc.vector.tensor_tensor(out=q[:], in0=q[:], in1=cos_t[:], op=ALU.mult)
+                for m in range(TOKEN_TILES):
                     nc.vector.tensor_tensor(
-                        out=q[:], in0=q[:], in1=mixed[:], op=(ALU.add if which == 0 else ALU.subtract)
+                        out=q_rows[m][:, span], in0=q_rows[m][:, span], in1=cos_t[:, span], op=ALU.mult
                     )
-                    nc.gpsimd.dma_start(out=rows, in_=q[:])
+            if cc == CHUNKS_PER_OUTPUT - 1:
+                for m in range(TOKEN_TILES):
+                    nc.vector.tensor_tensor(
+                        out=q_rows[m][:], in0=q_rows[m][:], in1=mixed[m][:],
+                        op=(ALU.add if which == 0 else ALU.subtract),
+                    )
+                    nc.gpsimd.dma_start(out=out_rows[which][m * P : (m + 1) * P, :], in_=q_rows[m][:])
 
         def multiply(slab):
             c, part = divmod(slab, SLABS_PER_CHUNK)
@@ -261,7 +273,10 @@ def tile_rotaryembeddingtransformerlayer_pa_kernel(
                         stop=(g == PASSES - 1),
                     )
             if part == SLABS_PER_CHUNK - 1:
-                finish(c)
+                if c < 2 * CHUNKS_PER_OUTPUT:
+                    finish_q_or_k(c)
+                else:
+                    finish_v(c)
 
         for slab in range(SLABS_AHEAD, SLABS + SLABS_AHEAD):
             multiply(slab - SLABS_AHEAD)

@@ -52,7 +52,6 @@ def tile_rotaryembeddingtransformerlayer_pa_kernel(
     out_rows = [out_q.flatten_outer_dims(), out_k.flatten_outer_dims(), out_v.flatten_outer_dims()]
 
     with ExitStack() as pools:
-        pools.enter_context(tc.manual_schedule())
         const = pools.enter_context(tc.tile_pool(name="const", bufs=1))
         w_pool = pools.enter_context(tc.tile_pool(name="w_raw", bufs=W_BUFS))
         grouped_pool = pools.enter_context(tc.tile_pool(name="grouped", bufs=SLABS_AHEAD))

import math
from contextlib import ExitStack

import concourse.mybir as mybir
from concourse.masks import make_identity

F32 = mybir.dt.float32
BF16 = mybir.dt.bfloat16
U32 = mybir.dt.uint32
U8 = mybir.dt.uint8
FP8X4 = mybir.dt.float8_e4m3fn_x4
ALU = mybir.AluOpType
ACT = mybir.ActivationFunctionType

P = 128
TOKENS = 256
POSITIONS = 64
TOKEN_TILES = TOKENS // P
D = 2048
E = 2048
HALF_E = E // 2
EPS = 1e-5

PACK = 4
K_PASS = P * PACK
PASSES = D // K_PASS
WORDS_PER_PASS = K_PASS // 2

CHUNK = 512
ROW_TILES = CHUNK // P
CHUNKS = 3 * E // CHUNK
CHUNKS_PER_OUTPUT = E // CHUNK
SLAB_PASSES = 2
SLABS_PER_CHUNK = PASSES // SLAB_PASSES
SLABS = CHUNKS * SLABS_PER_CHUNK
SLABS_AHEAD = 4
SLABS_BEFORE_X = 2
W_BUFS = 4

ROUND = 1.5 * 2.0**23
FREQ_RATIO = 10000.0 ** (-1.0 / HALF_E)
REDUCED = HALF_E // 2

FLOPS = 2 * TOKENS * D * 3 * E


def tile_rotaryembeddingtransformerlayer_pa_kernel(
    tc, src, Wqkv, bqkv, g1, be1, out_q, out_k, out_v
):
    nc = tc.nc
    x_rows = src.flatten_outer_dims()
    out_rows = [out_q.flatten_outer_dims(), out_k.flatten_outer_dims(), out_v.flatten_outer_dims()]

    with ExitStack() as pools:
        const = pools.enter_context(tc.tile_pool(name="const", bufs=1))
        w_pool = pools.enter_context(tc.tile_pool(name="w_raw", bufs=W_BUFS))
        grouped_pool = pools.enter_context(tc.tile_pool(name="grouped", bufs=SLABS_AHEAD))
        code_pool = pools.enter_context(tc.tile_pool(name="codes", bufs=SLABS_AHEAD + 2))
        psum_tr = pools.enter_context(tc.psum_pool(name="psum_tr", bufs=4))
        psum_acc = pools.enter_context(tc.psum_pool(name="psum_acc", bufs=4))

        ident = const.tile([P, P], F32)
        bias_bc = const.tile([P, 3 * E], BF16)
        x_codes = const.tile([P, PASSES * TOKENS], U32, align_bytes=64)
        x_scales = const.tile([P, PASSES * TOKENS], U8, align_bytes=64)
        cos_t = const.tile([P, E], F32)
        sin_t = const.tile([P, E], F32)

        w_raw = {}
        w_codes = {}
        w_scales = {}
        acc = {}
        q_rows = {}
        mixed = {}

        def load_chunk(c):
            w_raw[c] = w_pool.tile([P, ROW_TILES, D], BF16, name="w_raw")
            nc.sync.dma_start(
                out=w_raw[c][:],
                in_=Wqkv[c * CHUNK : (c + 1) * CHUNK, :].rearrange("(p t) k -> p t k", t=ROW_TILES),
            )
            if c % CHUNKS_PER_OUTPUT == 0:
                span = slice(c * CHUNK, c * CHUNK + E)
                nc.sync.dma_start(out=bias_bc[:, span], in_=bqkv[span].partition_broadcast(P))

        def transpose_words(rows_of, g, width, dest_words):
            w_t = psum_tr.tile([P, 2, width], F32, name="w_t", tag="tr")
            for j in range(width // P):
                words = rows_of(j).bitcast(F32)
                for u in range(2):
                    w0 = g * WORDS_PER_PASS + u * P
                    nc.tensor.transpose(w_t[:, u, j * P : (j + 1) * P], words[:, w0 : w0 + P], ident[:])
            nc.scalar.copy(out=dest_words, in_=w_t[:].rearrange("p u n -> p n u"))

        def prepare(slab):
            c, part = divmod(slab, SLABS_PER_CHUNK)
            grouped = grouped_pool.tile(
                [P, SLAB_PASSES * CHUNK * PACK], BF16, name="grouped", align_bytes=64
            )
            grouped_words = grouped[:].bitcast(F32).rearrange("p (i n u) -> p i n u", i=SLAB_PASSES, u=2)
            for i in range(SLAB_PASSES):
                for h in range(2):
                    transpose_words(
                        lambda j: w_raw[c][:, 2 * h + j, :],
                        part * SLAB_PASSES + i,
                        2 * P,
                        grouped_words[:, i, h * 2 * P : (h + 1) * 2 * P, :],
                    )
            w_codes[slab] = code_pool.tile([P, SLAB_PASSES * CHUNK], U32, name="w_codes", align_bytes=64)
            w_scales[slab] = code_pool.tile([P, SLAB_PASSES * CHUNK], U8, name="w_scales", align_bytes=64)
            nc.vector.quantize_mx(
                out=w_codes[slab][:].bitcast(FP8X4), scales=w_scales[slab][:], in_=grouped[:]
            )
            if part == SLABS_PER_CHUNK - 1 and c + W_BUFS < CHUNKS:
                load_chunk(c + W_BUFS)

        with tc.tile_pool(name="head", bufs=1) as head:
            x_raw = []
            for m in range(TOKEN_TILES):
                x_raw.append(head.tile([P, D], BF16, name="x_raw%d" % m))
                nc.sync.dma_start(out=x_raw[m][:], in_=x_rows[m * P : (m + 1) * P, :])
            gain_bc = head.tile([P, D], BF16)
            nc.sync.dma_start(out=gain_bc[:], in_=g1.partition_broadcast(P))
            shift_bc = head.tile([P, D], BF16)
            nc.sync.dma_start(out=shift_bc[:], in_=be1.partition_broadcast(P))
            for c in range(W_BUFS):
                load_chunk(c)

            pos = head.tile([P, 1], F32)
            for first in range(0, P, POSITIONS):
                nc.gpsimd.iota(
                    pos[first : first + POSITIONS, :],
                    pattern=[[0, 1]],
                    base=0,
                    channel_multiplier=1,
                    allow_small_or_imprecise_dtypes=True,
                )
            turns = head.tile([P, HALF_E], F32)
            nc.gpsimd.tensor_scalar(
                out=turns[:, 0:1], in0=pos[:], scalar1=1.0 / (2.0 * math.pi), scalar2=0.0,
                op0=ALU.mult, op1=ALU.add,
            )
            make_identity(nc, ident[:])
            n = 1
            while n < HALF_E:
                nc.vector.tensor_scalar(
                    out=turns[:, n : 2 * n], in0=turns[:, 0:n], scalar1=FREQ_RATIO**n, scalar2=None,
                    op0=ALU.mult,
                )
                n *= 2
            whole = head.tile([P, REDUCED], F32)
            nc.vector.tensor_scalar(
                out=whole[:], in0=turns[:, 0:REDUCED], scalar1=ROUND, scalar2=ROUND,
                op0=ALU.add, op1=ALU.subtract,
            )
            nc.vector.tensor_tensor(
                out=turns[:, 0:REDUCED], in0=turns[:, 0:REDUCED], in1=whole[:], op=ALU.subtract
            )
            abs_turns = head.tile([P, HALF_E], F32)
            nc.vector.scalar_tensor_tensor(
                out=abs_turns[:], in0=turns[:], scalar=-1.0, in1=turns[:], op0=ALU.mult, op1=ALU.max
            )
            nc.scalar.activation(out=cos_t[:, 0:HALF_E], in_=turns[:], func=ACT.Sin, scale=2.0 * math.pi)
            nc.scalar.activation(
                out=cos_t[:, HALF_E:E], in_=abs_turns[:], func=ACT.Sin,
                scale=-2.0 * math.pi, bias=math.pi / 2.0,
            )
            nc.scalar.activation(out=sin_t[:, 0:HALF_E], in_=cos_t[:, 0:HALF_E], func=ACT.Sin, scale=-1.0)
            nc.scalar.activation(out=sin_t[:, HALF_E:E], in_=cos_t[:, HALF_E:E], func=ACT.Sin)
            nc.scalar.activation(out=cos_t[:], in_=cos_t[:], func=ACT.Sin, bias=math.pi / 2.0)

            mean_var = head.tile([P, TOKEN_TILES, 2], F32)
            for m in range(TOKEN_TILES):
                stats = head.tile([P, D // 512, 6], F32, name="stats%d" % m)
                for j in range(D // 512):
                    nc.vector.bn_stats(out=stats[:, j, :], in_=x_raw[m][:, j * 512 : (j + 1) * 512])
                nc.vector.bn_aggr(out=mean_var[:, m, :], in_=stats[:].rearrange("p c s -> p (c s)"))
            std = head.tile([P, TOKEN_TILES], F32)
            nc.scalar.activation(out=std[:], in_=mean_var[:, :, 1], func=ACT.Sqrt, bias=EPS)
            centred = []
            for m in range(TOKEN_TILES):
                centred.append(head.tile([P, D], F32, name="centred%d" % m))
                nc.vector.scalar_tensor_tensor(
                    out=centred[m][:], in0=x_raw[m][:], scalar=mean_var[:, m, 0:1], in1=gain_bc[:],
                    op0=ALU.subtract, op1=ALU.mult,
                )
            rstd = head.tile([P, TOKEN_TILES], F32)
            nc.vector.reciprocal(out=rstd[:], in_=std[:])
            xn = []
            for m in range(TOKEN_TILES):
                xn.append(head.tile([P, D], BF16, name="xn%d" % m))
                nc.vector.scalar_tensor_tensor(
                    out=xn[m][:], in0=centred[m][:], scalar=rstd[:, m : m + 1], in1=shift_bc[:],
                    op0=ALU.mult, op1=ALU.add,
                )

            for slab in range(SLABS_BEFORE_X):
                prepare(slab)

            grouped_x = head.tile([P, PASSES * TOKENS * PACK], BF16, align_bytes=64)
            grouped_x_words = grouped_x[:].bitcast(F32).rearrange("p (g r u) -> p g r u", g=PASSES, u=2)
            for g in range(PASSES):
                transpose_words(lambda m: xn[m][:], g, TOKENS, grouped_x_words[:, g, :, :])
            nc.vector.quantize_mx(out=x_codes[:].bitcast(FP8X4), scales=x_scales[:], in_=grouped_x[:])

            for slab in range(SLABS_BEFORE_X, SLABS_AHEAD):
                prepare(slab)

        rot = pools.enter_context(tc.tile_pool(name="rot", bufs=4))

        def add_bias(c, m, dest):
            nc.vector.tensor_tensor(
                out=dest.rearrange("r (p t) -> r p t", t=ROW_TILES),
                in0=acc[m][:].rearrange("r (t p) -> r p t", t=ROW_TILES),
                in1=bias_bc[:, c * CHUNK : (c + 1) * CHUNK].rearrange("r (p t) -> r p t", t=ROW_TILES),
                op=ALU.add,
            )

        def finish_v(c):
            cc = c % CHUNKS_PER_OUTPUT
            for m in range(TOKEN_TILES):
                v_rows = rot.tile([P, CHUNK], F32, name="v_rows")
                add_bias(c, m, v_rows[:])
                nc.sync.dma_start(
                    out=out_rows[2][m * P : (m + 1) * P, cc * CHUNK : (cc + 1) * CHUNK], in_=v_rows[:]
                )

        def finish_q_or_k(c):
            which, cc = divmod(c, CHUNKS_PER_OUTPUT)
            for m in range(TOKEN_TILES):
                if cc == 0:
                    q_rows[m] = rot.tile([P, E], F32, name="q_rows")
                    mixed[m] = rot.tile([P, E], F32, name="mixed", bufs=TOKEN_TILES)
                add_bias(c, m, q_rows[m][:, cc * CHUNK : (cc + 1) * CHUNK])
            if cc % 2 == 1:
                j = cc // 2
                span = slice(j * HALF_E, (j + 1) * HALF_E)
                for m in range(TOKEN_TILES):
                    nc.vector.tensor_tensor(
                        out=mixed[m][:].rearrange("r (h j i) -> r h j i", h=2, j=2)[:, :, j, :],
                        in0=q_rows[m][:, span].rearrange("r (i h) -> r h i", h=2),
                        in1=sin_t[:].rearrange("r (h j i) -> r h j i", h=2, j=2)[:, :, j, :],
                        op=ALU.mult,
                    )
                for m in range(TOKEN_TILES):
                    nc.vector.tensor_tensor(
                        out=q_rows[m][:, span], in0=q_rows[m][:, span], in1=cos_t[:, span], op=ALU.mult
                    )
            if cc == CHUNKS_PER_OUTPUT - 1:
                for m in range(TOKEN_TILES):
                    nc.vector.tensor_tensor(
                        out=q_rows[m][:], in0=q_rows[m][:], in1=mixed[m][:],
                        op=(ALU.add if which == 0 else ALU.subtract),
                    )
                    nc.gpsimd.dma_start(out=out_rows[which][m * P : (m + 1) * P, :], in_=q_rows[m][:])

        def multiply(slab):
            c, part = divmod(slab, SLABS_PER_CHUNK)
            for i in range(SLAB_PASSES):
                g = part * SLAB_PASSES + i
                for m in range(TOKEN_TILES):
                    if g == 0:
                        acc[m] = psum_acc.tile([P, CHUNK], F32, name="acc", tag="acc")
                    tokens = slice(g * TOKENS + m * P, g * TOKENS + (m + 1) * P)
                    nc.tensor.matmul_mx(
                        out=acc[m][:],
                        lhsT=x_codes[:, tokens].bitcast(FP8X4),
                        lhsT_scale=x_scales[:, tokens],
                        rhs=w_codes[slab][:, i * CHUNK : (i + 1) * CHUNK].bitcast(FP8X4),
                        rhs_scale=w_scales[slab][:, i * CHUNK : (i + 1) * CHUNK],
                        start=(g == 0),
                        stop=(g == PASSES - 1),
                    )
            if part == SLABS_PER_CHUNK - 1:
                if c < 2 * CHUNKS_PER_OUTPUT:
                    finish_q_or_k(c)
                else:
                    finish_v(c)

        for slab in range(SLABS_AHEAD, SLABS + SLABS_AHEAD):
            multiply(slab - SLABS_AHEAD)
            if slab < SLABS:
                prepare(slab)
